import numpy as np
import ml_dtypes


def mxq(x, axis, fmt="e4m3"):
    dtype, down = {"e4m3": (ml_dtypes.float8_e4m3fn, 7), "e5m2": (ml_dtypes.float8_e5m2, 14)}[fmt]
    v = np.moveaxis(np.asarray(x, np.float32).astype(ml_dtypes.bfloat16).astype(np.float64), axis, -1)
    blocks = v.reshape(v.shape[:-1] + (-1, 32))
    amax = np.abs(blocks).max(-1, keepdims=True)
    byte = np.maximum(np.where(amax > 0, np.frexp(amax)[1] - 1 + 127, 0) - down, 1)
    scale = np.exp2(byte - 127.0)
    codes = (blocks / scale).astype(np.float32).astype(dtype).astype(np.float64)
    return np.moveaxis((codes * scale).reshape(v.shape), -1, axis)


WIDE = False


def mx_kscale(k):
    if not WIDE:
        return np.ones(k)
    levels = np.array([10, -10, 5, -5, 0])
    a = np.random.permutation(np.resize(levels, k // 512 * 4)).reshape(k // 512, 4)
    idx = np.arange(k)
    return np.exp2(a[idx // 512, idx % 128 // 32])


BF16 = ml_dtypes.bfloat16


def bf(x):
    return np.asarray(x, np.float32).astype(BF16)


def f64(x):
    return np.asarray(x).astype(np.float64)


B, A, C, P = 64, 7, 512, 128
N = A * A + 1


def scramble(y):
    return y.transpose(0, 2, 1).reshape(B, N, C)


def unscramble(z):
    return z.reshape(B, C, N).transpose(0, 2, 1)


def setup_inputs():
    s = mx_kscale(C)
    z = np.random.standard_normal((B, N, C)) * 1.6 / np.sqrt(N) * s
    return {"y_attn": bf(np.ascontiguousarray(unscramble(z))),
            "w_proj": bf(np.random.standard_normal((P, C)) * 2.0 / np.sqrt(C) / s),
            "b_proj": bf(np.random.standard_normal(P) * 0.1)}


def reference(y_attn, w_proj, b_proj):
    z = scramble(f64(y_attn))
    return (mxq(z, 2, "e4m3") @ mxq(f64(w_proj), 1, "e4m3").T) + f64(b_proj)

@@ -1,0 +1,156 @@
+from contextlib import ExitStack
+
+import concourse.mybir as mybir
+from concourse.masks import make_identity
+
+F32 = mybir.dt.float32
+BF16 = mybir.dt.bfloat16
+U32 = mybir.dt.uint32
+U8 = mybir.dt.uint8
+FP8X4 = mybir.dt.float8_e4m3fn_x4
+
+P = 128
+IMAGES, TOKENS, CHANNELS, FEATURES = 64, 50, 512, 128
+PACK = 4
+HALVES = 2
+PARITIES = 2
+HALF_CHANNELS = CHANNELS // HALVES
+TOKEN_PAIRS = TOKENS // PARITIES
+ROWS = TOKENS // HALVES
+GROUPS = 2
+GROUP_IMAGES = IMAGES // GROUPS
+GROUP_COLUMNS = GROUP_IMAGES * HALVES
+ROW_WORDS = CHANNELS // PACK
+ROWS_PER_BANK = 4
+PIECE = 32
+RUN = 4
+
+FLOPS = 2 * IMAGES * TOKENS * CHANNELS * FEATURES
+
+
+def tile_attention_pa_s_kernel(tc, y_attn, w_proj, b_proj, out):
+    nc = tc.nc
+    row_tiles = [(r, min(ROWS_PER_BANK, ROWS - r)) for r in range(0, ROWS, ROWS_PER_BANK)]
+
+    with ExitStack() as stack:
+        consts = stack.enter_context(tc.tile_pool(name="consts", bufs=1))
+        data = stack.enter_context(tc.tile_pool(name="data", bufs=1))
+        turned_pool = stack.enter_context(tc.psum_pool(name="turned_pool", bufs=4))
+        sums_pool = stack.enter_context(tc.psum_pool(name="sums_pool", bufs=3))
+
+        w_rows = consts.tile([P, CHANNELS], BF16)
+        nc.scalar.dma_start(out=w_rows[:], in_=w_proj)
+        bias_rows = consts.tile([P, FEATURES], BF16)
+        nc.vector.memset(bias_rows[:], 0.0)
+        nc.scalar.dma_start(out=bias_rows[0:1, :], in_=b_proj.rearrange("(a o) -> a o", a=1))
+
+        y_parts = y_attn.rearrange(
+            "(g b) (n e) (h c) -> g h e b n c", g=GROUPS, e=PARITIES, h=HALVES
+        )
+        raw = [data.tile([P, TOKEN_PAIRS, HALF_CHANNELS], BF16, name="raw%d" % g) for g in range(GROUPS)]
+        for g in range(GROUPS):
+            for h in range(HALVES):
+                for e in range(PARITIES):
+                    first = PARITIES * h + e
+                    nc.sync.dma_start(
+                        out=raw[g][first : P : HALVES * PARITIES, :, :], in_=y_parts[g, h, e]
+                    )
+
+        identity = consts.tile([P, P], F32)
+        make_identity(nc, identity[:])
+        ones = consts.tile([P, P], BF16)
+        nc.vector.memset(ones[:], 1.0)
+
+        bias_sum = sums_pool.tile([P, ROWS_PER_BANK, FEATURES], F32, tag="sums")
+        nc.tensor.matmul(out=bias_sum[:, 0, :], lhsT=ones[:], rhs=bias_rows[:], start=True, stop=True)
+        bias = consts.tile([P, FEATURES], F32)
+        nc.vector.tensor_copy(out=bias[:], in_=bias_sum[:, 0, :])
+
+        w_split = consts.tile([P, PARITIES, CHANNELS // PARITIES], BF16)
+        nc.vector.tensor_copy(out=w_split[:], in_=w_rows[:].rearrange("o (m e) -> o e m", e=PARITIES))
+        w_turned = turned_pool.tile([P, ROWS_PER_BANK, ROW_WORDS], F32, tag="turned")
+        for e in range(PARITIES):
+            nc.tensor.transpose(w_turned[:, e, :], w_split[:, e, :].bitcast(F32), identity[:])
+        w_grouped = consts.tile([P, FEATURES * PACK], BF16, align_bytes=64)
+        nc.vector.tensor_copy(
+            out=w_grouped[:].bitcast(F32).rearrange("p (o e) -> p o e", e=PARITIES),
+            in_=w_turned[:, 0:PARITIES, :].rearrange("p e o -> p o e"),
+        )
+        w_codes = consts.tile([P, FEATURES], U32, align_bytes=64)
+        w_scales = consts.tile([P, FEATURES], U8, align_bytes=64)
+        nc.vector.quantize_mx(out=w_codes[:].bitcast(FP8X4), scales=w_scales[:], in_=w_grouped[:])
+
+        flat = [data.tile([P, HALF_CHANNELS * TOKEN_PAIRS], BF16, name="flat%d" % g) for g in range(GROUPS)]
+        grouped = data.tile([P, ROWS * GROUPS * GROUP_COLUMNS * PACK], BF16, align_bytes=64)
+        grouped_values = grouped[:].rearrange("p (r g v) -> p r g v", r=ROWS, g=GROUPS)
+        grouped_words = grouped[:].bitcast(F32).rearrange("p (r g w) -> p r g w", r=ROWS, g=GROUPS)
+        z_codes = data.tile([P, ROWS, GROUPS * GROUP_COLUMNS], U32, align_bytes=64)
+        z_scales = data.tile([P, ROWS, GROUPS * GROUP_COLUMNS], U8, align_bytes=64)
+        result = data.tile([P, ROWS, FEATURES], F32)
+        out_rows = out.rearrange("b (h r) o -> (b h) r o", h=HALVES)
+
+        def reorder(g, piece):
+            channels = slice(piece * PIECE, (piece + 1) * PIECE)
+            source = raw[g][:, :, channels].rearrange("p n (c i) -> p c n i", i=RUN)
+            by_channel = flat[g][:].rearrange("p (c n) -> p c n", n=TOKEN_PAIRS)
+            target = by_channel[:, channels, :].rearrange("p (c i) n -> p c n i", i=RUN)
+            if piece % 3 == 2:
+                nc.scalar.copy(out=target, in_=source)
+            else:
+                nc.vector.tensor_copy(out=target, in_=source)
+
+        def turn(g, first_row, rows):
+            words = flat[g][:].bitcast(F32)
+            turned = turned_pool.tile([P, ROWS_PER_BANK, ROW_WORDS], F32)
+            for k in range(rows):
+                start = (first_row + k) * ROW_WORDS
+                nc.tensor.transpose(turned[:, k, :], words[:, start : start + ROW_WORDS], identity[:])
+            nc.scalar.copy(
+                out=grouped_words[:, first_row : first_row + rows, g, :], in_=turned[:, 0:rows, :]
+            )
+
+        def quantise(g, first_row, rows):
+            columns = slice(g * GROUP_COLUMNS, (g + 1) * GROUP_COLUMNS)
+            for r in range(first_row, first_row + rows):
+                nc.vector.quantize_mx(
+                    out=z_codes[:, r, columns].bitcast(FP8X4),
+                    scales=z_scales[:, r, columns],
+                    in_=grouped_values[:, r, g, :],
+                )
+
+        def multiply(first_row, rows):
+            sums = sums_pool.tile([P, ROWS_PER_BANK, FEATURES], F32)
+            for k in range(rows):
+                nc.tensor.matmul_mx(
+                    out=sums[:, k, :],
+                    lhsT=z_codes[:, first_row + k, :].bitcast(FP8X4),
+                    lhsT_scale=z_scales[:, first_row + k, :],
+                    rhs=w_codes[:].bitcast(FP8X4),
+                    rhs_scale=w_scales[:],
+                    start=True,
+                    stop=True,
+                )
+            done = slice(first_row, first_row + rows)
+            nc.vector.tensor_tensor(
+                out=result[:, done, :],
+                in0=sums[:, 0:rows, :],
+                in1=bias[:].unsqueeze(1).to_broadcast([P, rows, FEATURES]),
+                op=mybir.AluOpType.add,
+            )
+            nc.sync.dma_start(out=out_rows[:, done, :], in_=result[:, done, :])
+
+        steps = len(row_tiles)
+        for g in range(GROUPS):
+            pieces_done = 0
+            for step in range(steps + 2):
+                if step < steps:
+                    first_row, rows = row_tiles[step]
+                    values_needed = (first_row + rows) * ROW_WORDS * 2
+                    while pieces_done * PIECE * TOKEN_PAIRS < values_needed:
+                        reorder(g, pieces_done)
+                        pieces_done += 1
+                    turn(g, first_row, rows)
+                if 1 <= step <= steps:
+                    quantise(g, *row_tiles[step - 1])
+                if g == GROUPS - 1 and step >= 2:
+                    multiply(*row_tiles[step - 2])

@@ -19,10 +19,16 @@ TOKEN_PAIRS = TOKENS // PARITIES
 ROWS = TOKENS // HALVES
 GROUPS = 2
 GROUP_IMAGES = IMAGES // GROUPS
-GROUP_COLUMNS = GROUP_IMAGES * HALVES
-ROW_WORDS = CHANNELS // PACK
-ROWS_PER_BANK = 4
-PIECE = 32
+ROW_COLUMNS = GROUP_IMAGES * HALVES
+ROW_VALUES = CHANNELS // PARITIES
+ROW_WORDS = ROW_VALUES // 2
+ROW_SETS = 2
+PASSES = (ROWS + 1) // ROW_SETS
+PASS_VALUES = P * PACK
+BANK_PASSES = 2
+STEP_PASSES = 4
+FIRST_PAIRS = 13
+VECTOR_CHANNELS, SCALAR_CHANNELS = 32, 16
 RUN = 4
 
 FLOPS = 2 * IMAGES * TOKENS * CHANNELS * FEATURES
@@ -30,13 +36,15 @@ FLOPS = 2 * IMAGES * TOKENS * CHANNELS * FEATURES
 
 def tile_attention_pa_s_kernel(tc, y_attn, w_proj, b_proj, out):
     nc = tc.nc
-    row_tiles = [(r, min(ROWS_PER_BANK, ROWS - r)) for r in range(0, ROWS, ROWS_PER_BANK)]
+    steps = [(k, min(STEP_PASSES, PASSES - k)) for k in range(0, PASSES, STEP_PASSES)]
+    parts = [slice(0, FIRST_PAIRS), slice(FIRST_PAIRS, TOKEN_PAIRS)]
 
     with ExitStack() as stack:
         consts = stack.enter_context(tc.tile_pool(name="consts", bufs=1))
         data = stack.enter_context(tc.tile_pool(name="data", bufs=1))
         turned_pool = stack.enter_context(tc.psum_pool(name="turned_pool", bufs=4))
-        sums_pool = stack.enter_context(tc.psum_pool(name="sums_pool", bufs=3))
+        sums_pool = stack.enter_context(tc.psum_pool(name="sums_pool", bufs=2))
+        stack.enter_context(tc.manual_schedule())
 
         w_rows = consts.tile([P, CHANNELS], BF16)
         nc.scalar.dma_start(out=w_rows[:], in_=w_proj)
@@ -49,108 +57,125 @@ def tile_attention_pa_s_kernel(tc, y_attn, w_proj, b_proj, out):
         )
         raw = [data.tile([P, TOKEN_PAIRS, HALF_CHANNELS], BF16, name="raw%d" % g) for g in range(GROUPS)]
         for g in range(GROUPS):
-            for h in range(HALVES):
-                for e in range(PARITIES):
-                    first = PARITIES * h + e
-                    nc.sync.dma_start(
-                        out=raw[g][first : P : HALVES * PARITIES, :, :], in_=y_parts[g, h, e]
-                    )
+            for pairs in parts:
+                for h in range(HALVES):
+                    for e in range(PARITIES):
+                        nc.sync.dma_start(
+                            out=raw[g][PARITIES * h + e : P : HALVES * PARITIES, pairs, :],
+                            in_=y_parts[g, h, e][:, pairs, :],
+                        )
 
         identity = consts.tile([P, P], F32)
         make_identity(nc, identity[:])
         ones = consts.tile([P, P], BF16)
         nc.vector.memset(ones[:], 1.0)
+        flat = [data.tile([P, ROW_SETS * PASSES * ROW_VALUES], BF16, name="flat%d" % g) for g in range(GROUPS)]
+        for g in range(GROUPS):
+            nc.vector.memset(flat[g][:, ROWS * ROW_VALUES :], 0.0)
 
-        bias_sum = sums_pool.tile([P, ROWS_PER_BANK, FEATURES], F32, tag="sums")
+        bias_sum = sums_pool.tile([P, STEP_PASSES, FEATURES], F32, tag="sums")
         nc.tensor.matmul(out=bias_sum[:, 0, :], lhsT=ones[:], rhs=bias_rows[:], start=True, stop=True)
         bias = consts.tile([P, FEATURES], F32)
         nc.vector.tensor_copy(out=bias[:], in_=bias_sum[:, 0, :])
 
-        w_split = consts.tile([P, PARITIES, CHANNELS // PARITIES], BF16)
+        w_split = consts.tile([P, PARITIES, ROW_VALUES], BF16)
         nc.vector.tensor_copy(out=w_split[:], in_=w_rows[:].rearrange("o (m e) -> o e m", e=PARITIES))
-        w_turned = turned_pool.tile([P, ROWS_PER_BANK, ROW_WORDS], F32, tag="turned")
+        w_turned = turned_pool.tile([P, ROW_SETS, BANK_PASSES, ROW_WORDS], F32, tag="turned")
         for e in range(PARITIES):
-            nc.tensor.transpose(w_turned[:, e, :], w_split[:, e, :].bitcast(F32), identity[:])
-        w_grouped = consts.tile([P, FEATURES * PACK], BF16, align_bytes=64)
+            nc.tensor.transpose(w_turned[:, e, 0, :], w_split[:, e, :].bitcast(F32), identity[:])
+        w_grouped = consts.tile([P, PASS_VALUES], BF16, align_bytes=64)
         nc.vector.tensor_copy(
             out=w_grouped[:].bitcast(F32).rearrange("p (o e) -> p o e", e=PARITIES),
-            in_=w_turned[:, 0:PARITIES, :].rearrange("p e o -> p o e"),
+            in_=w_turned[:, :, 0, :].rearrange("p e o -> p o e"),
         )
         w_codes = consts.tile([P, FEATURES], U32, align_bytes=64)
         w_scales = consts.tile([P, FEATURES], U8, align_bytes=64)
         nc.vector.quantize_mx(out=w_codes[:].bitcast(FP8X4), scales=w_scales[:], in_=w_grouped[:])
 
-        flat = [data.tile([P, HALF_CHANNELS * TOKEN_PAIRS], BF16, name="flat%d" % g) for g in range(GROUPS)]
-        grouped = data.tile([P, ROWS * GROUPS * GROUP_COLUMNS * PACK], BF16, align_bytes=64)
-        grouped_values = grouped[:].rearrange("p (r g v) -> p r g v", r=ROWS, g=GROUPS)
-        grouped_words = grouped[:].bitcast(F32).rearrange("p (r g w) -> p r g w", r=ROWS, g=GROUPS)
-        z_codes = data.tile([P, ROWS, GROUPS * GROUP_COLUMNS], U32, align_bytes=64)
-        z_scales = data.tile([P, ROWS, GROUPS * GROUP_COLUMNS], U8, align_bytes=64)
-        result = data.tile([P, ROWS, FEATURES], F32)
-        out_rows = out.rearrange("b (h r) o -> (b h) r o", h=HALVES)
+        grouped = [data.tile([P, PASSES * PASS_VALUES], BF16, name="grouped%d" % g, align_bytes=64) for g in range(GROUPS)]
+        z_codes = [data.tile([P, PASSES * P], U32, name="z_codes%d" % g, align_bytes=64) for g in range(GROUPS)]
+        z_scales = [data.tile([P, PASSES * P], U8, name="z_scales%d" % g, align_bytes=64) for g in range(GROUPS)]
+        result = [data.tile([P, PASSES, FEATURES], F32, name="result%d" % g) for g in range(GROUPS)]
+        out_rows = out.rearrange("(g b) (h r) o -> g (b h) r o", g=GROUPS, h=HALVES)
 
-        def reorder(g, piece):
-            channels = slice(piece * PIECE, (piece + 1) * PIECE)
-            source = raw[g][:, :, channels].rearrange("p n (c i) -> p c n i", i=RUN)
-            by_channel = flat[g][:].rearrange("p (c n) -> p c n", n=TOKEN_PAIRS)
-            target = by_channel[:, channels, :].rearrange("p (c i) n -> p c n i", i=RUN)
-            if piece % 3 == 2:
-                nc.scalar.copy(out=target, in_=source)
-            else:
+        def reorder(g, pairs):
+            by_channel = flat[g][:, 0 : ROWS * ROW_VALUES].rearrange("p (c n) -> p c n", n=TOKEN_PAIRS)
+
+            def views(first, last):
+                source = raw[g][:, pairs, first:last].rearrange("p n (c i) -> p c n i", i=RUN)
+                target = by_channel[:, first:last, pairs].rearrange("p (c i) n -> p c n i", i=RUN)
+                return target, source
+
+            for first in range(0, HALF_CHANNELS, VECTOR_CHANNELS + SCALAR_CHANNELS):
+                middle = min(first + VECTOR_CHANNELS, HALF_CHANNELS)
+                last = min(middle + SCALAR_CHANNELS, HALF_CHANNELS)
+                target, source = views(first, middle)
                 nc.vector.tensor_copy(out=target, in_=source)
+                if last > middle:
+                    target, source = views(middle, last)
+                    nc.scalar.copy(out=target, in_=source)
 
-        def turn(g, first_row, rows):
+        def turn(g, first_pass, passes):
             words = flat[g][:].bitcast(F32)
-            turned = turned_pool.tile([P, ROWS_PER_BANK, ROW_WORDS], F32)
-            for k in range(rows):
-                start = (first_row + k) * ROW_WORDS
-                nc.tensor.transpose(turned[:, k, :], words[:, start : start + ROW_WORDS], identity[:])
-            nc.scalar.copy(
-                out=grouped_words[:, first_row : first_row + rows, g, :], in_=turned[:, 0:rows, :]
+            packed = grouped[g][:].bitcast(F32).rearrange(
+                "p (k c q e) -> p k c q e", c=ROW_COLUMNS, q=ROW_SETS, e=PARITIES
             )
-
-        def quantise(g, first_row, rows):
-            columns = slice(g * GROUP_COLUMNS, (g + 1) * GROUP_COLUMNS)
-            for r in range(first_row, first_row + rows):
-                nc.vector.quantize_mx(
-                    out=z_codes[:, r, columns].bitcast(FP8X4),
-                    scales=z_scales[:, r, columns],
-                    in_=grouped_values[:, r, g, :],
+            for k0 in range(first_pass, first_pass + passes, BANK_PASSES):
+                count = min(BANK_PASSES, first_pass + passes - k0)
+                turned = turned_pool.tile([P, ROW_SETS, BANK_PASSES, ROW_WORDS], F32)
+                for q in range(ROW_SETS):
+                    for k in range(count):
+                        start = (q * PASSES + k0 + k) * ROW_WORDS
+                        nc.tensor.transpose(turned[:, q, k, :], words[:, start : start + ROW_WORDS], identity[:])
+                nc.scalar.copy(
+                    out=packed[:, k0 : k0 + count].rearrange("p k c q e -> p (k c) q e"),
+                    in_=turned[:, :, 0:count, :].rearrange("p q k (c e) -> p (k c) q e", e=PARITIES),
                 )
 
-        def multiply(first_row, rows):
-            sums = sums_pool.tile([P, ROWS_PER_BANK, FEATURES], F32)
-            for k in range(rows):
+        def quantise(g, first_pass, passes):
+            nc.vector.quantize_mx(
+                out=z_codes[g][:, first_pass * P : (first_pass + passes) * P].bitcast(FP8X4),
+                scales=z_scales[g][:, first_pass * P : (first_pass + passes) * P],
+                in_=grouped[g][:, first_pass * PASS_VALUES : (first_pass + passes) * PASS_VALUES],
+            )
+
+        def multiply(g, first_pass, passes):
+            sums = sums_pool.tile([P, STEP_PASSES, FEATURES], F32)
+            for k in range(passes):
+                columns = slice((first_pass + k) * P, (first_pass + k + 1) * P)
                 nc.tensor.matmul_mx(
                     out=sums[:, k, :],
-                    lhsT=z_codes[:, first_row + k, :].bitcast(FP8X4),
-                    lhsT_scale=z_scales[:, first_row + k, :],
+                    lhsT=z_codes[g][:, columns].bitcast(FP8X4),
+                    lhsT_scale=z_scales[g][:, columns],
                     rhs=w_codes[:].bitcast(FP8X4),
                     rhs_scale=w_scales[:],
                     start=True,
                     stop=True,
                 )
-            done = slice(first_row, first_row + rows)
             nc.vector.tensor_tensor(
-                out=result[:, done, :],
-                in0=sums[:, 0:rows, :],
-                in1=bias[:].unsqueeze(1).to_broadcast([P, rows, FEATURES]),
+                out=result[g][:, first_pass : first_pass + passes, :],
+                in0=sums[:, 0:passes, :],
+                in1=bias[:].unsqueeze(1).to_broadcast([P, passes, FEATURES]),
                 op=mybir.AluOpType.add,
             )
-            nc.sync.dma_start(out=out_rows[:, done, :], in_=result[:, done, :])
+            for q in range(ROW_SETS):
+                first_row = q * PASSES + first_pass
+                rows = min(passes, ROWS - first_row)
+                if rows > 0:
+                    nc.sync.dma_start(
+                        out=out_rows[g][:, first_row : first_row + rows, :],
+                        in_=result[g][q:P:ROW_SETS, first_pass : first_pass + rows, :],
+                    )
 
-        steps = len(row_tiles)
+        reorder(0, parts[0])
         for g in range(GROUPS):
-            pieces_done = 0
-            for step in range(steps + 2):
-                if step < steps:
-                    first_row, rows = row_tiles[step]
-                    values_needed = (first_row + rows) * ROW_WORDS * 2
-                    while pieces_done * PIECE * TOKEN_PAIRS < values_needed:
-                        reorder(g, pieces_done)
-                        pieces_done += 1
-                    turn(g, first_row, rows)
-                if 1 <= step <= steps:
-                    quantise(g, *row_tiles[step - 1])
-                if g == GROUPS - 1 and step >= 2:
-                    multiply(*row_tiles[step - 2])
+            reorder(g, parts[1])
+            for i in range(len(steps) + 2):
+                if i < len(steps):
+                    turn(g, *steps[i])
+                if 1 <= i <= len(steps):
+                    quantise(g, *steps[i - 1])
+                if i >= 2:
+                    multiply(g, *steps[i - 2])
+                if i == 1 and g + 1 < GROUPS:
+                    reorder(g + 1, parts[0])

@@ -28,7 +28,10 @@ PASS_VALUES = P * PACK
 BANK_PASSES = 2
 STEP_PASSES = 4
 FIRST_PAIRS = 13
-VECTOR_CHANNELS, SCALAR_CHANNELS = 32, 16
+VECTOR_CHANNELS, SCALAR_CHANNELS = 48, 16
+QUANTISE_LAG = 1
+MULTIPLY_LAG = 3
+STEP_BUFFERS = 5
 RUN = 4
 
 FLOPS = 2 * IMAGES * TOKENS * CHANNELS * FEATURES
@@ -37,13 +40,14 @@ FLOPS = 2 * IMAGES * TOKENS * CHANNELS * FEATURES
 def tile_attention_pa_s_kernel(tc, y_attn, w_proj, b_proj, out):
     nc = tc.nc
     steps = [(k, min(STEP_PASSES, PASSES - k)) for k in range(0, PASSES, STEP_PASSES)]
-    parts = [slice(0, FIRST_PAIRS), slice(FIRST_PAIRS, TOKEN_PAIRS)]
+    parts = [(0, FIRST_PAIRS), (FIRST_PAIRS, TOKEN_PAIRS)]
 
     with ExitStack() as stack:
         consts = stack.enter_context(tc.tile_pool(name="consts", bufs=1))
         data = stack.enter_context(tc.tile_pool(name="data", bufs=1))
-        turned_pool = stack.enter_context(tc.psum_pool(name="turned_pool", bufs=4))
-        sums_pool = stack.enter_context(tc.psum_pool(name="sums_pool", bufs=2))
+        step_pool = stack.enter_context(tc.tile_pool(name="step_pool", bufs=STEP_BUFFERS))
+        turned_pool = stack.enter_context(tc.psum_pool(name="turned_pool", bufs=5))
+        sums_pool = stack.enter_context(tc.psum_pool(name="sums_pool", bufs=3))
         stack.enter_context(tc.manual_schedule())
 
         w_rows = consts.tile([P, CHANNELS], BF16)
@@ -55,14 +59,17 @@ def tile_attention_pa_s_kernel(tc, y_attn, w_proj, b_proj, out):
         y_parts = y_attn.rearrange(
             "(g b) (n e) (h c) -> g h e b n c", g=GROUPS, e=PARITIES, h=HALVES
         )
-        raw = [data.tile([P, TOKEN_PAIRS, HALF_CHANNELS], BF16, name="raw%d" % g) for g in range(GROUPS)]
+        raw = {}
         for g in range(GROUPS):
-            for pairs in parts:
+            for part, (first_pair, last_pair) in enumerate(parts):
+                raw[g, part] = data.tile(
+                    [P, last_pair - first_pair, HALF_CHANNELS], BF16, name="raw%d%d" % (g, part)
+                )
                 for h in range(HALVES):
                     for e in range(PARITIES):
                         nc.sync.dma_start(
-                            out=raw[g][PARITIES * h + e : P : HALVES * PARITIES, pairs, :],
-                            in_=y_parts[g, h, e][:, pairs, :],
+                            out=raw[g, part][PARITIES * h + e : P : HALVES * PARITIES, :, :],
+                            in_=y_parts[g, h, e][:, first_pair:last_pair, :],
                         )
 
         identity = consts.tile([P, P], F32)
@@ -92,17 +99,16 @@ def tile_attention_pa_s_kernel(tc, y_attn, w_proj, b_proj, out):
         w_scales = consts.tile([P, FEATURES], U8, align_bytes=64)
         nc.vector.quantize_mx(out=w_codes[:].bitcast(FP8X4), scales=w_scales[:], in_=w_grouped[:])
 
-        grouped = [data.tile([P, PASSES * PASS_VALUES], BF16, name="grouped%d" % g, align_bytes=64) for g in range(GROUPS)]
-        z_codes = [data.tile([P, PASSES * P], U32, name="z_codes%d" % g, align_bytes=64) for g in range(GROUPS)]
-        z_scales = [data.tile([P, PASSES * P], U8, name="z_scales%d" % g, align_bytes=64) for g in range(GROUPS)]
-        result = [data.tile([P, PASSES, FEATURES], F32, name="result%d" % g) for g in range(GROUPS)]
+        grouped_of = {}
+        operand_of = {}
         out_rows = out.rearrange("(g b) (h r) o -> g (b h) r o", g=GROUPS, h=HALVES)
 
-        def reorder(g, pairs):
+        def reorder(g, part):
+            pairs = slice(*parts[part])
             by_channel = flat[g][:, 0 : ROWS * ROW_VALUES].rearrange("p (c n) -> p c n", n=TOKEN_PAIRS)
 
             def views(first, last):
-                source = raw[g][:, pairs, first:last].rearrange("p n (c i) -> p c n i", i=RUN)
+                source = raw[g, part][:, :, first:last].rearrange("p n (c i) -> p c n i", i=RUN)
                 target = by_channel[:, first:last, pairs].rearrange("p (c i) n -> p c n i", i=RUN)
                 return target, source
 
@@ -117,15 +123,17 @@ def tile_attention_pa_s_kernel(tc, y_attn, w_proj, b_proj, out):
 
         def turn(g, first_pass, passes):
             words = flat[g][:].bitcast(F32)
-            packed = grouped[g][:].bitcast(F32).rearrange(
+            grouped = step_pool.tile([P, STEP_PASSES * PASS_VALUES], BF16, align_bytes=64)
+            grouped_of[g, first_pass] = grouped
+            packed = grouped[:].bitcast(F32).rearrange(
                 "p (k c q e) -> p k c q e", c=ROW_COLUMNS, q=ROW_SETS, e=PARITIES
             )
-            for k0 in range(first_pass, first_pass + passes, BANK_PASSES):
-                count = min(BANK_PASSES, first_pass + passes - k0)
+            for k0 in range(0, passes, BANK_PASSES):
+                count = min(BANK_PASSES, passes - k0)
                 turned = turned_pool.tile([P, ROW_SETS, BANK_PASSES, ROW_WORDS], F32)
                 for q in range(ROW_SETS):
                     for k in range(count):
-                        start = (q * PASSES + k0 + k) * ROW_WORDS
+                        start = (q * PASSES + first_pass + k0 + k) * ROW_WORDS
                         nc.tensor.transpose(turned[:, q, k, :], words[:, start : start + ROW_WORDS], identity[:])
                 nc.scalar.copy(
                     out=packed[:, k0 : k0 + count].rearrange("p k c q e -> p (k c) q e"),
@@ -133,27 +141,32 @@ def tile_attention_pa_s_kernel(tc, y_attn, w_proj, b_proj, out):
                 )
 
         def quantise(g, first_pass, passes):
+            codes = step_pool.tile([P, STEP_PASSES * P], U32, align_bytes=64)
+            scales = step_pool.tile([P, STEP_PASSES * P], U8, align_bytes=64)
+            operand_of[g, first_pass] = (codes, scales)
             nc.vector.quantize_mx(
-                out=z_codes[g][:, first_pass * P : (first_pass + passes) * P].bitcast(FP8X4),
-                scales=z_scales[g][:, first_pass * P : (first_pass + passes) * P],
-                in_=grouped[g][:, first_pass * PASS_VALUES : (first_pass + passes) * PASS_VALUES],
+                out=codes[:, 0 : passes * P].bitcast(FP8X4),
+                scales=scales[:, 0 : passes * P],
+                in_=grouped_of[g, first_pass][:, 0 : passes * PASS_VALUES],
             )
 
         def multiply(g, first_pass, passes):
+            codes, scales = operand_of[g, first_pass]
             sums = sums_pool.tile([P, STEP_PASSES, FEATURES], F32)
             for k in range(passes):
-                columns = slice((first_pass + k) * P, (first_pass + k + 1) * P)
+                columns = slice(k * P, (k + 1) * P)
                 nc.tensor.matmul_mx(
                     out=sums[:, k, :],
-                    lhsT=z_codes[g][:, columns].bitcast(FP8X4),
-                    lhsT_scale=z_scales[g][:, columns],
+                    lhsT=codes[:, columns].bitcast(FP8X4),
+                    lhsT_scale=scales[:, columns],
                     rhs=w_codes[:].bitcast(FP8X4),
                     rhs_scale=w_scales[:],
                     start=True,
                     stop=True,
                 )
+            result = step_pool.tile([P, STEP_PASSES, FEATURES], F32)
             nc.vector.tensor_tensor(
-                out=result[g][:, first_pass : first_pass + passes, :],
+                out=result[:, 0:passes, :],
                 in0=sums[:, 0:passes, :],
                 in1=bias[:].unsqueeze(1).to_broadcast([P, passes, FEATURES]),
                 op=mybir.AluOpType.add,
@@ -164,18 +177,19 @@ def tile_attention_pa_s_kernel(tc, y_attn, w_proj, b_proj, out):
                 if rows > 0:
                     nc.sync.dma_start(
                         out=out_rows[g][:, first_row : first_row + rows, :],
-                        in_=result[g][q:P:ROW_SETS, first_pass : first_pass + rows, :],
+                        in_=result[q:P:ROW_SETS, 0:rows, :],
                     )
 
-        reorder(0, parts[0])
-        for g in range(GROUPS):
-            reorder(g, parts[1])
-            for i in range(len(steps) + 2):
-                if i < len(steps):
-                    turn(g, *steps[i])
-                if 1 <= i <= len(steps):
-                    quantise(g, *steps[i - 1])
-                if i >= 2:
-                    multiply(g, *steps[i - 2])
-                if i == 1 and g + 1 < GROUPS:
-                    reorder(g + 1, parts[0])
+        work = [(g, first_pass, passes) for g in range(GROUPS) for first_pass, passes in steps]
+        for part in range(len(parts)):
+            reorder(0, part)
+        for i in range(len(work) + MULTIPLY_LAG):
+            if i < len(work):
+                turn(*work[i])
+            if 0 <= i - QUANTISE_LAG < len(work):
+                quantise(*work[i - QUANTISE_LAG])
+            if i >= MULTIPLY_LAG:
+                multiply(*work[i - MULTIPLY_LAG])
+            g, step = divmod(i, len(steps))
+            if g + 1 < GROUPS and step < len(parts):
+                reorder(g + 1, step)

@@ -33,6 +33,9 @@ QUANTISE_LAG = 1
 MULTIPLY_LAG = 3
 STEP_BUFFERS = 5
 RUN = 4
+WARM_MATMULS = 2
+WARM_PASSES = 6
+KEEP_PASSES = 2
 
 FLOPS = 2 * IMAGES * TOKENS * CHANNELS * FEATURES
 
@@ -150,9 +153,34 @@ def tile_attention_pa_s_kernel(tc, y_attn, w_proj, b_proj, out):
                 in_=grouped_of[g, first_pass][:, 0 : passes * PASS_VALUES],
             )
 
+        def idle_passes(target, count):
+            for k in range(count):
+                nc.tensor.matmul_mx(
+                    out=target,
+                    lhsT=w_codes[:].bitcast(FP8X4),
+                    lhsT_scale=w_scales[:],
+                    rhs=w_codes[:].bitcast(FP8X4),
+                    rhs_scale=w_scales[:],
+                    start=True,
+                    stop=True,
+                )
+
+        def warm_up():
+            sums = sums_pool.tile([P, STEP_PASSES, FEATURES], F32)
+            for k in range(WARM_MATMULS):
+                nc.tensor.matmul(
+                    out=sums[:].rearrange("p k o -> p (k o)"),
+                    lhsT=ones[:],
+                    rhs=raw[0, len(parts) - 1][:, 2 * k : 2 * k + 2, :].rearrange("p n c -> p (n c)"),
+                    start=True,
+                    stop=True,
+                )
+            idle_passes(sums[:, 0, :], WARM_PASSES)
+
         def multiply(g, first_pass, passes):
             codes, scales = operand_of[g, first_pass]
             sums = sums_pool.tile([P, STEP_PASSES, FEATURES], F32)
+            idle_passes(sums[:, 0, :], KEEP_PASSES)
             for k in range(passes):
                 columns = slice(k * P, (k + 1) * P)
                 nc.tensor.matmul_mx(
@@ -183,6 +211,7 @@ def tile_attention_pa_s_kernel(tc, y_attn, w_proj, b_proj, out):
         work = [(g, first_pass, passes) for g in range(GROUPS) for first_pass, passes in steps]
         for part in range(len(parts)):
             reorder(0, part)
+        warm_up()
         for i in range(len(work) + MULTIPLY_LAG):
             if i < len(work):
                 turn(*work[i])

@@ -23,12 +23,14 @@ ROW_COLUMNS = GROUP_IMAGES * HALVES
 ROW_VALUES = CHANNELS // PARITIES
 ROW_WORDS = ROW_VALUES // 2
 ROW_SETS = 2
-PASSES = (ROWS + 1) // ROW_SETS
+PASSES = ROWS // ROW_SETS
+MIDDLE_ROW = PASSES
+UPPER_ROW = MIDDLE_ROW + 1
 PASS_VALUES = P * PACK
 BANK_PASSES = 2
 STEP_PASSES = 4
 FIRST_PAIRS = 13
-VECTOR_CHANNELS, SCALAR_CHANNELS = 48, 16
+VECTOR_CHANNELS, SCALAR_CHANNELS = 52, 12
 QUANTISE_LAG = 1
 MULTIPLY_LAG = 3
 STEP_BUFFERS = 5
@@ -42,7 +44,11 @@ FLOPS = 2 * IMAGES * TOKENS * CHANNELS * FEATURES
 
 def tile_attention_pa_s_kernel(tc, y_attn, w_proj, b_proj, out):
     nc = tc.nc
-    steps = [(k, min(STEP_PASSES, PASSES - k)) for k in range(0, PASSES, STEP_PASSES)]
+    steps = [
+        (STEP_PASSES, ((g, k), (g, UPPER_ROW + k))) for g in range(GROUPS) for k in range(0, PASSES, STEP_PASSES)
+    ]
+    steps.append((1, tuple((g, MIDDLE_ROW) for g in range(GROUPS))))
+    group_steps = PASSES // STEP_PASSES
     parts = [(0, FIRST_PAIRS), (FIRST_PAIRS, TOKEN_PAIRS)]
 
     with ExitStack() as stack:
@@ -56,7 +62,7 @@ def tile_attention_pa_s_kernel(tc, y_attn, w_proj, b_proj, out):
         w_rows = consts.tile([P, CHANNELS], BF16)
         nc.scalar.dma_start(out=w_rows[:], in_=w_proj)
         bias_rows = consts.tile([P, FEATURES], BF16)
-        nc.vector.memset(bias_rows[:], 0.0)
+        nc.gpsimd.memset(bias_rows[:], 0.0)
         nc.scalar.dma_start(out=bias_rows[0:1, :], in_=b_proj.rearrange("(a o) -> a o", a=1))
 
         y_parts = y_attn.rearrange(
@@ -78,29 +84,26 @@ def tile_attention_pa_s_kernel(tc, y_attn, w_proj, b_proj, out):
         identity = consts.tile([P, P], F32)
         make_identity(nc, identity[:])
         ones = consts.tile([P, P], BF16)
-        nc.vector.memset(ones[:], 1.0)
-        flat = [data.tile([P, ROW_SETS * PASSES * ROW_VALUES], BF16, name="flat%d" % g) for g in range(GROUPS)]
-        for g in range(GROUPS):
-            nc.vector.memset(flat[g][:, ROWS * ROW_VALUES :], 0.0)
+        nc.gpsimd.memset(ones[:], 1.0)
+        flat = [data.tile([P, ROWS * ROW_VALUES], BF16, name="flat%d" % g) for g in range(GROUPS)]
 
         bias_sum = sums_pool.tile([P, STEP_PASSES, FEATURES], F32, tag="sums")
         nc.tensor.matmul(out=bias_sum[:, 0, :], lhsT=ones[:], rhs=bias_rows[:], start=True, stop=True)
         bias = consts.tile([P, FEATURES], F32)
-        nc.vector.tensor_copy(out=bias[:], in_=bias_sum[:, 0, :])
+        nc.scalar.copy(out=bias[:], in_=bias_sum[:, 0, :])
 
         w_split = consts.tile([P, PARITIES, ROW_VALUES], BF16)
-        nc.vector.tensor_copy(out=w_split[:], in_=w_rows[:].rearrange("o (m e) -> o e m", e=PARITIES))
+        nc.scalar.copy(out=w_split[:], in_=w_rows[:].rearrange("o (m e) -> o e m", e=PARITIES))
         w_turned = turned_pool.tile([P, ROW_SETS, BANK_PASSES, ROW_WORDS], F32, tag="turned")
         for e in range(PARITIES):
             nc.tensor.transpose(w_turned[:, e, 0, :], w_split[:, e, :].bitcast(F32), identity[:])
         w_grouped = consts.tile([P, PASS_VALUES], BF16, align_bytes=64)
-        nc.vector.tensor_copy(
+        nc.scalar.copy(
             out=w_grouped[:].bitcast(F32).rearrange("p (o e) -> p o e", e=PARITIES),
             in_=w_turned[:, :, 0, :].rearrange("p e o -> p o e"),
         )
         w_codes = consts.tile([P, FEATURES], U32, align_bytes=64)
         w_scales = consts.tile([P, FEATURES], U8, align_bytes=64)
-        nc.vector.quantize_mx(out=w_codes[:].bitcast(FP8X4), scales=w_scales[:], in_=w_grouped[:])
 
         grouped_of = {}
         operand_of = {}
@@ -108,14 +111,16 @@ def tile_attention_pa_s_kernel(tc, y_attn, w_proj, b_proj, out):
 
         def reorder(g, part):
             pairs = slice(*parts[part])
-            by_channel = flat[g][:, 0 : ROWS * ROW_VALUES].rearrange("p (c n) -> p c n", n=TOKEN_PAIRS)
+            by_channel = flat[g][:].rearrange("p (c n) -> p c n", n=TOKEN_PAIRS)
 
             def views(first, last):
                 source = raw[g, part][:, :, first:last].rearrange("p n (c i) -> p c n i", i=RUN)
                 target = by_channel[:, first:last, pairs].rearrange("p (c i) n -> p c n i", i=RUN)
                 return target, source
 
-            for first in range(0, HALF_CHANNELS, VECTOR_CHANNELS + SCALAR_CHANNELS):
+            chunk = VECTOR_CHANNELS + SCALAR_CHANNELS
+            half = HALF_CHANNELS // ROW_SETS
+            for first in [q * half + c for c in range(0, half, chunk) for q in range(ROW_SETS)]:
                 middle = min(first + VECTOR_CHANNELS, HALF_CHANNELS)
                 last = min(middle + SCALAR_CHANNELS, HALF_CHANNELS)
                 target, source = views(first, middle)
@@ -124,33 +129,35 @@ def tile_attention_pa_s_kernel(tc, y_attn, w_proj, b_proj, out):
                     target, source = views(middle, last)
                     nc.scalar.copy(out=target, in_=source)
 
-        def turn(g, first_pass, passes):
-            words = flat[g][:].bitcast(F32)
+        def turn(step):
+            passes, sources = step
             grouped = step_pool.tile([P, STEP_PASSES * PASS_VALUES], BF16, align_bytes=64)
-            grouped_of[g, first_pass] = grouped
+            grouped_of[step] = grouped
             packed = grouped[:].bitcast(F32).rearrange(
                 "p (k c q e) -> p k c q e", c=ROW_COLUMNS, q=ROW_SETS, e=PARITIES
             )
             for k0 in range(0, passes, BANK_PASSES):
                 count = min(BANK_PASSES, passes - k0)
                 turned = turned_pool.tile([P, ROW_SETS, BANK_PASSES, ROW_WORDS], F32)
-                for q in range(ROW_SETS):
+                for q, (g, first_row) in enumerate(sources):
+                    words = flat[g][:].bitcast(F32)
                     for k in range(count):
-                        start = (q * PASSES + first_pass + k0 + k) * ROW_WORDS
+                        start = (first_row + k0 + k) * ROW_WORDS
                         nc.tensor.transpose(turned[:, q, k, :], words[:, start : start + ROW_WORDS], identity[:])
                 nc.scalar.copy(
                     out=packed[:, k0 : k0 + count].rearrange("p k c q e -> p (k c) q e"),
                     in_=turned[:, :, 0:count, :].rearrange("p q k (c e) -> p (k c) q e", e=PARITIES),
                 )
 
-        def quantise(g, first_pass, passes):
+        def quantise(step):
+            passes = step[0]
             codes = step_pool.tile([P, STEP_PASSES * P], U32, align_bytes=64)
             scales = step_pool.tile([P, STEP_PASSES * P], U8, align_bytes=64)
-            operand_of[g, first_pass] = (codes, scales)
+            operand_of[step] = (codes, scales)
             nc.vector.quantize_mx(
                 out=codes[:, 0 : passes * P].bitcast(FP8X4),
                 scales=scales[:, 0 : passes * P],
-                in_=grouped_of[g, first_pass][:, 0 : passes * PASS_VALUES],
+                in_=grouped_of[step][:, 0 : passes * PASS_VALUES],
             )
 
         def idle_passes(target, count):
@@ -177,8 +184,9 @@ def tile_attention_pa_s_kernel(tc, y_attn, w_proj, b_proj, out):
                 )
             idle_passes(sums[:, 0, :], WARM_PASSES)
 
-        def multiply(g, first_pass, passes):
-            codes, scales = operand_of[g, first_pass]
+        def multiply(step):
+            passes, sources = step
+            codes, scales = operand_of[step]
             sums = sums_pool.tile([P, STEP_PASSES, FEATURES], F32)
             idle_passes(sums[:, 0, :], KEEP_PASSES)
             for k in range(passes):
@@ -199,26 +207,24 @@ def tile_attention_pa_s_kernel(tc, y_attn, w_proj, b_proj, out):
                 in1=bias[:].unsqueeze(1).to_broadcast([P, passes, FEATURES]),
                 op=mybir.AluOpType.add,
             )
-            for q in range(ROW_SETS):
-                first_row = q * PASSES + first_pass
-                rows = min(passes, ROWS - first_row)
-                if rows > 0:
-                    nc.sync.dma_start(
-                        out=out_rows[g][:, first_row : first_row + rows, :],
-                        in_=result[q:P:ROW_SETS, 0:rows, :],
-                    )
+            for q, (g, first_row) in enumerate(sources):
+                nc.sync.dma_start(
+                    out=out_rows[g][:, first_row : first_row + passes, :],
+                    in_=result[q:P:ROW_SETS, 0:passes, :],
+                )
 
-        work = [(g, first_pass, passes) for g in range(GROUPS) for first_pass, passes in steps]
         for part in range(len(parts)):
             reorder(0, part)
+            if part == 0:
+                nc.vector.quantize_mx(out=w_codes[:].bitcast(FP8X4), scales=w_scales[:], in_=w_grouped[:])
         warm_up()
-        for i in range(len(work) + MULTIPLY_LAG):
-            if i < len(work):
-                turn(*work[i])
-            if 0 <= i - QUANTISE_LAG < len(work):
-                quantise(*work[i - QUANTISE_LAG])
+        for i in range(len(steps) + MULTIPLY_LAG):
+            if i < len(steps):
+                turn(steps[i])
+            if 0 <= i - QUANTISE_LAG < len(steps):
+                quantise(steps[i - QUANTISE_LAG])
             if i >= MULTIPLY_LAG:
-                multiply(*work[i - MULTIPLY_LAG])
-            g, step = divmod(i, len(steps))
-            if g + 1 < GROUPS and step < len(parts):
-                reorder(g + 1, step)
+                multiply(steps[i - MULTIPLY_LAG])
+            g, part = divmod(i, group_steps)
+            if g + 1 < GROUPS and part < len(parts):
+                reorder(g + 1, part)

@@ -30,7 +30,8 @@ PASS_VALUES = P * PACK
 BANK_PASSES = 2
 STEP_PASSES = 4
 FIRST_PAIRS = 13
-VECTOR_CHANNELS, SCALAR_CHANNELS = 52, 12
+CHUNK_CHANNELS = 64
+SCALAR_CHANNELS = (64, 0)
 QUANTISE_LAG = 1
 MULTIPLY_LAG = 3
 STEP_BUFFERS = 5
@@ -118,16 +119,19 @@ def tile_attention_pa_s_kernel(tc, y_attn, w_proj, b_proj, out):
                 target = by_channel[:, first:last, pairs].rearrange("p (c i) n -> p c n i", i=RUN)
                 return target, source
 
-            chunk = VECTOR_CHANNELS + SCALAR_CHANNELS
-            half = HALF_CHANNELS // ROW_SETS
-            for first in [q * half + c for c in range(0, half, chunk) for q in range(ROW_SETS)]:
-                middle = min(first + VECTOR_CHANNELS, HALF_CHANNELS)
-                last = min(middle + SCALAR_CHANNELS, HALF_CHANNELS)
-                target, source = views(first, middle)
+            vector_channels = HALF_CHANNELS - SCALAR_CHANNELS[g]
+            if SCALAR_CHANNELS[g] > 0:
+                target, source = views(vector_channels, HALF_CHANNELS)
+                nc.scalar.copy(out=target, in_=source)
+            if part + 1 < len(parts):
+                chunks = [(0, vector_channels)]
+            else:
+                half = HALF_CHANNELS // ROW_SETS
+                firsts = [q * half + c for c in range(0, half, CHUNK_CHANNELS) for q in range(ROW_SETS)]
+                chunks = [(first, first + CHUNK_CHANNELS) for first in firsts if first < vector_channels]
+            for first, last in chunks:
+                target, source = views(first, last)
                 nc.vector.tensor_copy(out=target, in_=source)
-                if last > middle:
-                    target, source = views(middle, last)
-                    nc.scalar.copy(out=target, in_=source)
 
         def turn(step):
             passes, sources = step
@@ -178,7 +182,7 @@ def tile_attention_pa_s_kernel(tc, y_attn, w_proj, b_proj, out):
                 nc.tensor.matmul(
                     out=sums[:].rearrange("p k o -> p (k o)"),
                     lhsT=ones[:],
-                    rhs=raw[0, len(parts) - 1][:, 2 * k : 2 * k + 2, :].rearrange("p n c -> p (n c)"),
+                    rhs=raw[0, 0][:, 2 * k : 2 * k + 2, :].rearrange("p n c -> p (n c)"),
                     start=True,
                     stop=True,
                 )

@@ -31,7 +31,7 @@ BANK_PASSES = 2
 STEP_PASSES = 4
 FIRST_PAIRS = 13
 CHUNK_CHANNELS = 64
-SCALAR_CHANNELS = (64, 0)
+SCALAR_CHANNELS = (64, 64)
 QUANTISE_LAG = 1
 MULTIPLY_LAG = 3
 STEP_BUFFERS = 5

@@ -223,12 +223,12 @@ def tile_attention_pa_s_kernel(tc, y_attn, w_proj, b_proj, out):
                 nc.vector.quantize_mx(out=w_codes[:].bitcast(FP8X4), scales=w_scales[:], in_=w_grouped[:])
         warm_up()
         for i in range(len(steps) + MULTIPLY_LAG):
+            if i >= MULTIPLY_LAG:
+                multiply(steps[i - MULTIPLY_LAG])
             if i < len(steps):
                 turn(steps[i])
             if 0 <= i - QUANTISE_LAG < len(steps):
                 quantise(steps[i - QUANTISE_LAG])
-            if i >= MULTIPLY_LAG:
-                multiply(steps[i - MULTIPLY_LAG])
             g, part = divmod(i, group_steps)
             if g + 1 < GROUPS and part < len(parts):
                 reorder(g + 1, part)

@@ -30,7 +30,7 @@ PASS_VALUES = P * PACK
 BANK_PASSES = 2
 STEP_PASSES = 4
 FIRST_PAIRS = 13
-CHUNK_CHANNELS = 64
+FIRST_CHANNELS = 48
 SCALAR_CHANNELS = (64, 64)
 QUANTISE_LAG = 1
 MULTIPLY_LAG = 3
@@ -88,21 +88,20 @@ def tile_attention_pa_s_kernel(tc, y_attn, w_proj, b_proj, out):
         nc.gpsimd.memset(ones[:], 1.0)
         flat = [data.tile([P, ROWS * ROW_VALUES], BF16, name="flat%d" % g) for g in range(GROUPS)]
 
+        w_turned = turned_pool.tile([P, ROW_SETS * BANK_PASSES * ROW_WORDS], F32, tag="turned")
+        for u in range(PARITIES):
+            nc.tensor.transpose(
+                w_turned[:, u * P : (u + 1) * P], w_rows[:].bitcast(F32)[:, u::PARITIES], identity[:]
+            )
+        w_grouped = consts.tile([P, PASS_VALUES], BF16, align_bytes=64)
+        nc.scalar.copy(
+            out=w_grouped[:].rearrange("p (o e u) -> p o e u", e=PARITIES, u=PARITIES),
+            in_=w_turned[:, 0 : PARITIES * P].bitcast(BF16).rearrange("p (u o e) -> p o e u", u=PARITIES, e=PARITIES),
+        )
+
         bias_sum = sums_pool.tile([P, STEP_PASSES, FEATURES], F32, tag="sums")
         nc.tensor.matmul(out=bias_sum[:, 0, :], lhsT=ones[:], rhs=bias_rows[:], start=True, stop=True)
         bias = consts.tile([P, FEATURES], F32)
-        nc.scalar.copy(out=bias[:], in_=bias_sum[:, 0, :])
-
-        w_split = consts.tile([P, PARITIES, ROW_VALUES], BF16)
-        nc.scalar.copy(out=w_split[:], in_=w_rows[:].rearrange("o (m e) -> o e m", e=PARITIES))
-        w_turned = turned_pool.tile([P, ROW_SETS, BANK_PASSES, ROW_WORDS], F32, tag="turned")
-        for e in range(PARITIES):
-            nc.tensor.transpose(w_turned[:, e, 0, :], w_split[:, e, :].bitcast(F32), identity[:])
-        w_grouped = consts.tile([P, PASS_VALUES], BF16, align_bytes=64)
-        nc.scalar.copy(
-            out=w_grouped[:].bitcast(F32).rearrange("p (o e) -> p o e", e=PARITIES),
-            in_=w_turned[:, :, 0, :].rearrange("p e o -> p o e"),
-        )
         w_codes = consts.tile([P, FEATURES], U32, align_bytes=64)
         w_scales = consts.tile([P, FEATURES], U8, align_bytes=64)
 
@@ -127,8 +126,8 @@ def tile_attention_pa_s_kernel(tc, y_attn, w_proj, b_proj, out):
                 chunks = [(0, vector_channels)]
             else:
                 half = HALF_CHANNELS // ROW_SETS
-                firsts = [q * half + c for c in range(0, half, CHUNK_CHANNELS) for q in range(ROW_SETS)]
-                chunks = [(first, first + CHUNK_CHANNELS) for first in firsts if first < vector_channels]
+                chunks = [(0, FIRST_CHANNELS), (half, half + FIRST_CHANNELS)]
+                chunks += [(FIRST_CHANNELS, half), (half + FIRST_CHANNELS, vector_channels)]
             for first, last in chunks:
                 target, source = views(first, last)
                 nc.vector.tensor_copy(out=target, in_=source)
@@ -142,7 +141,8 @@ def tile_attention_pa_s_kernel(tc, y_attn, w_proj, b_proj, out):
             )
             for k0 in range(0, passes, BANK_PASSES):
                 count = min(BANK_PASSES, passes - k0)
-                turned = turned_pool.tile([P, ROW_SETS, BANK_PASSES, ROW_WORDS], F32)
+                turned_bank = turned_pool.tile([P, ROW_SETS * BANK_PASSES * ROW_WORDS], F32, tag="turned")
+                turned = turned_bank[:].rearrange("p (q k w) -> p q k w", q=ROW_SETS, k=BANK_PASSES)
                 for q, (g, first_row) in enumerate(sources):
                     words = flat[g][:].bitcast(F32)
                     for k in range(count):
@@ -221,6 +221,7 @@ def tile_attention_pa_s_kernel(tc, y_attn, w_proj, b_proj, out):
             reorder(0, part)
             if part == 0:
                 nc.vector.quantize_mx(out=w_codes[:].bitcast(FP8X4), scales=w_scales[:], in_=w_grouped[:])
+                nc.scalar.copy(out=bias[:], in_=bias_sum[:, 0, :])
         warm_up()
         for i in range(len(steps) + MULTIPLY_LAG):
             if i >= MULTIPLY_LAG:

@@ -37,8 +37,9 @@ MULTIPLY_LAG = 3
 STEP_BUFFERS = 5
 RUN = 4
 WARM_MATMULS = 2
-WARM_PASSES = 6
-KEEP_PASSES = 2
+WARM_PASSES = 24
+HOLD_PASSES = 8
+KEEP_PASSES = 4
 
 FLOPS = 2 * IMAGES * TOKENS * CHANNELS * FEATURES
 
@@ -182,11 +183,15 @@ def tile_attention_pa_s_kernel(tc, y_attn, w_proj, b_proj, out):
                 nc.tensor.matmul(
                     out=sums[:].rearrange("p k o -> p (k o)"),
                     lhsT=ones[:],
-                    rhs=raw[0, 0][:, 2 * k : 2 * k + 2, :].rearrange("p n c -> p (n c)"),
+                    rhs=w_rows[:],
                     start=True,
                     stop=True,
                 )
             idle_passes(sums[:, 0, :], WARM_PASSES)
+
+        def hold():
+            sums = sums_pool.tile([P, STEP_PASSES, FEATURES], F32)
+            idle_passes(sums[:, 0, :], HOLD_PASSES)
 
         def multiply(step):
             passes, sources = step
@@ -217,10 +222,10 @@ def tile_attention_pa_s_kernel(tc, y_attn, w_proj, b_proj, out):
                     in_=result[q:P:ROW_SETS, 0:passes, :],
                 )
 
+        nc.vector.quantize_mx(out=w_codes[:].bitcast(FP8X4), scales=w_scales[:], in_=w_grouped[:])
         for part in range(len(parts)):
             reorder(0, part)
             if part == 0:
-                nc.vector.quantize_mx(out=w_codes[:].bitcast(FP8X4), scales=w_scales[:], in_=w_grouped[:])
                 nc.scalar.copy(out=bias[:], in_=bias_sum[:, 0, :])
         warm_up()
         for i in range(len(steps) + MULTIPLY_LAG):
@@ -228,6 +233,8 @@ def tile_attention_pa_s_kernel(tc, y_attn, w_proj, b_proj, out):
                 multiply(steps[i - MULTIPLY_LAG])
             if i < len(steps):
                 turn(steps[i])
+            if i < MULTIPLY_LAG:
+                hold()
             if 0 <= i - QUANTISE_LAG < len(steps):
                 quantise(steps[i - QUANTISE_LAG])
             g, part = divmod(i, group_steps)

@@ -37,9 +37,8 @@ MULTIPLY_LAG = 3
 STEP_BUFFERS = 5
 RUN = 4
 WARM_MATMULS = 2
-WARM_PASSES = 24
+WARM_PASSES = 18
 HOLD_PASSES = 8
-KEEP_PASSES = 4
 
 FLOPS = 2 * IMAGES * TOKENS * CHANNELS * FEATURES
 
@@ -165,10 +164,15 @@ def tile_attention_pa_s_kernel(tc, y_attn, w_proj, b_proj, out):
                 in_=grouped_of[step][:, 0 : passes * PASS_VALUES],
             )
 
-        def idle_passes(target, count):
+        spare = []
+
+        def idle_passes(count):
+            if not spare:
+                sums = sums_pool.tile([P, STEP_PASSES, FEATURES], F32)
+                spare.append(sums)
             for k in range(count):
                 nc.tensor.matmul_mx(
-                    out=target,
+                    out=spare[0][:, 0, :],
                     lhsT=w_codes[:].bitcast(FP8X4),
                     lhsT_scale=w_scales[:],
                     rhs=w_codes[:].bitcast(FP8X4),
@@ -181,23 +185,16 @@ def tile_attention_pa_s_kernel(tc, y_attn, w_proj, b_proj, out):
             sums = sums_pool.tile([P, STEP_PASSES, FEATURES], F32)
             for k in range(WARM_MATMULS):
                 nc.tensor.matmul(
-                    out=sums[:].rearrange("p k o -> p (k o)"),
-                    lhsT=ones[:],
-                    rhs=w_rows[:],
-                    start=True,
-                    stop=True,
+                    out=sums[:].rearrange("p k o -> p (k o)"), lhsT=ones[:], rhs=w_rows[:], start=True, stop=True
                 )
-            idle_passes(sums[:, 0, :], WARM_PASSES)
-
-        def hold():
-            sums = sums_pool.tile([P, STEP_PASSES, FEATURES], F32)
-            idle_passes(sums[:, 0, :], HOLD_PASSES)
+            spare.append(sums)
+            idle_passes(WARM_PASSES)
 
         def multiply(step):
             passes, sources = step
             codes, scales = operand_of[step]
-            sums = sums_pool.tile([P, STEP_PASSES, FEATURES], F32)
-            idle_passes(sums[:, 0, :], KEEP_PASSES)
+            idle_passes(0)
+            sums = spare.pop()
             for k in range(passes):
                 columns = slice(k * P, (k + 1) * P)
                 nc.tensor.matmul_mx(
@@ -233,8 +230,7 @@ def tile_attention_pa_s_kernel(tc, y_attn, w_proj, b_proj, out):
                 multiply(steps[i - MULTIPLY_LAG])
             if i < len(steps):
                 turn(steps[i])
-            if i < MULTIPLY_LAG:
-                hold()
+                idle_passes(HOLD_PASSES - (STEP_PASSES if i >= MULTIPLY_LAG else 0))
             if 0 <= i - QUANTISE_LAG < len(steps):
                 quantise(steps[i - QUANTISE_LAG])
             g, part = divmod(i, group_steps)

from contextlib import ExitStack

import concourse.mybir as mybir
from concourse.masks import make_identity

F32 = mybir.dt.float32
BF16 = mybir.dt.bfloat16
U32 = mybir.dt.uint32
U8 = mybir.dt.uint8
FP8X4 = mybir.dt.float8_e4m3fn_x4

P = 128
IMAGES, TOKENS, CHANNELS, FEATURES = 64, 50, 512, 128
PACK = 4
HALVES = 2
PARITIES = 2
HALF_CHANNELS = CHANNELS // HALVES
TOKEN_PAIRS = TOKENS // PARITIES
ROWS = TOKENS // HALVES
GROUPS = 2
GROUP_IMAGES = IMAGES // GROUPS
ROW_COLUMNS = GROUP_IMAGES * HALVES
ROW_VALUES = CHANNELS // PARITIES
ROW_WORDS = ROW_VALUES // 2
ROW_SETS = 2
PASSES = ROWS // ROW_SETS
MIDDLE_ROW = PASSES
UPPER_ROW = MIDDLE_ROW + 1
PASS_VALUES = P * PACK
BANK_PASSES = 2
STEP_PASSES = 4
FIRST_PAIRS = 13
FIRST_CHANNELS = 48
SCALAR_CHANNELS = (64, 64)
QUANTISE_LAG = 1
MULTIPLY_LAG = 3
STEP_BUFFERS = 5
RUN = 4
WARM_MATMULS = 2
WARM_PASSES = 18
HOLD_PASSES = 8

FLOPS = 2 * IMAGES * TOKENS * CHANNELS * FEATURES


def tile_attention_pa_s_kernel(tc, y_attn, w_proj, b_proj, out):
    nc = tc.nc
    steps = [
        (STEP_PASSES, ((g, k), (g, UPPER_ROW + k))) for g in range(GROUPS) for k in range(0, PASSES, STEP_PASSES)
    ]
    steps.append((1, tuple((g, MIDDLE_ROW) for g in range(GROUPS))))
    group_steps = PASSES // STEP_PASSES
    parts = [(0, FIRST_PAIRS), (FIRST_PAIRS, TOKEN_PAIRS)]

    with ExitStack() as stack:
        consts = stack.enter_context(tc.tile_pool(name="consts", bufs=1))
        data = stack.enter_context(tc.tile_pool(name="data", bufs=1))
        step_pool = stack.enter_context(tc.tile_pool(name="step_pool", bufs=STEP_BUFFERS))
        turned_pool = stack.enter_context(tc.psum_pool(name="turned_pool", bufs=5))
        sums_pool = stack.enter_context(tc.psum_pool(name="sums_pool", bufs=3))
        stack.enter_context(tc.manual_schedule())

        w_rows = consts.tile([P, CHANNELS], BF16)
        nc.scalar.dma_start(out=w_rows[:], in_=w_proj)
        bias_rows = consts.tile([P, FEATURES], BF16)
        nc.gpsimd.memset(bias_rows[:], 0.0)
        nc.scalar.dma_start(out=bias_rows[0:1, :], in_=b_proj.rearrange("(a o) -> a o", a=1))

        y_parts = y_attn.rearrange(
            "(g b) (n e) (h c) -> g h e b n c", g=GROUPS, e=PARITIES, h=HALVES
        )
        raw = {}
        for g in range(GROUPS):
            for part, (first_pair, last_pair) in enumerate(parts):
                raw[g, part] = data.tile(
                    [P, last_pair - first_pair, HALF_CHANNELS], BF16, name="raw%d%d" % (g, part)
                )
                for h in range(HALVES):
                    for e in range(PARITIES):
                        nc.sync.dma_start(
                            out=raw[g, part][PARITIES * h + e : P : HALVES * PARITIES, :, :],
                            in_=y_parts[g, h, e][:, first_pair:last_pair, :],
                        )

        identity = consts.tile([P, P], F32)
        make_identity(nc, identity[:])
        ones = consts.tile([P, P], BF16)
        nc.gpsimd.memset(ones[:], 1.0)
        flat = [data.tile([P, ROWS * ROW_VALUES], BF16, name="flat%d" % g) for g in range(GROUPS)]

        w_turned = turned_pool.tile([P, ROW_SETS * BANK_PASSES * ROW_WORDS], F32, tag="turned")
        for u in range(PARITIES):
            nc.tensor.transpose(
                w_turned[:, u * P : (u + 1) * P], w_rows[:].bitcast(F32)[:, u::PARITIES], identity[:]
            )
        w_grouped = consts.tile([P, PASS_VALUES], BF16, align_bytes=64)
        nc.scalar.copy(
            out=w_grouped[:].rearrange("p (o e u) -> p o e u", e=PARITIES, u=PARITIES),
            in_=w_turned[:, 0 : PARITIES * P].bitcast(BF16).rearrange("p (u o e) -> p o e u", u=PARITIES, e=PARITIES),
        )

        bias_sum = sums_pool.tile([P, STEP_PASSES, FEATURES], F32, tag="sums")
        nc.tensor.matmul(out=bias_sum[:, 0, :], lhsT=ones[:], rhs=bias_rows[:], start=True, stop=True)
        bias = consts.tile([P, FEATURES], F32)
        w_codes = consts.tile([P, FEATURES], U32, align_bytes=64)
        w_scales = consts.tile([P, FEATURES], U8, align_bytes=64)

        grouped_of = {}
        operand_of = {}
        out_rows = out.rearrange("(g b) (h r) o -> g (b h) r o", g=GROUPS, h=HALVES)

        def reorder(g, part):
            pairs = slice(*parts[part])
            by_channel = flat[g][:].rearrange("p (c n) -> p c n", n=TOKEN_PAIRS)

            def views(first, last):
                source = raw[g, part][:, :, first:last].rearrange("p n (c i) -> p c n i", i=RUN)
                target = by_channel[:, first:last, pairs].rearrange("p (c i) n -> p c n i", i=RUN)
                return target, source

            vector_channels = HALF_CHANNELS - SCALAR_CHANNELS[g]
            if SCALAR_CHANNELS[g] > 0:
                target, source = views(vector_channels, HALF_CHANNELS)
                nc.scalar.copy(out=target, in_=source)
            if part + 1 < len(parts):
                chunks = [(0, vector_channels)]
            else:
                half = HALF_CHANNELS // ROW_SETS
                chunks = [(0, FIRST_CHANNELS), (half, half + FIRST_CHANNELS)]
                chunks += [(FIRST_CHANNELS, half), (half + FIRST_CHANNELS, vector_channels)]
            for first, last in chunks:
                target, source = views(first, last)
                nc.vector.tensor_copy(out=target, in_=source)

        def turn(step):
            passes, sources = step
            grouped = step_pool.tile([P, STEP_PASSES * PASS_VALUES], BF16, align_bytes=64)
            grouped_of[step] = grouped
            packed = grouped[:].bitcast(F32).rearrange(
                "p (k c q e) -> p k c q e", c=ROW_COLUMNS, q=ROW_SETS, e=PARITIES
            )
            for k0 in range(0, passes, BANK_PASSES):
                count = min(BANK_PASSES, passes - k0)
                turned_bank = turned_pool.tile([P, ROW_SETS * BANK_PASSES * ROW_WORDS], F32, tag="turned")
                turned = turned_bank[:].rearrange("p (q k w) -> p q k w", q=ROW_SETS, k=BANK_PASSES)
                for q, (g, first_row) in enumerate(sources):
                    words = flat[g][:].bitcast(F32)
                    for k in range(count):
                        start = (first_row + k0 + k) * ROW_WORDS
                        nc.tensor.transpose(turned[:, q, k, :], words[:, start : start + ROW_WORDS], identity[:])
                nc.scalar.copy(
                    out=packed[:, k0 : k0 + count].rearrange("p k c q e -> p (k c) q e"),
                    in_=turned[:, :, 0:count, :].rearrange("p q k (c e) -> p (k c) q e", e=PARITIES),
                )

        def quantise(step):
            passes = step[0]
            codes = step_pool.tile([P, STEP_PASSES * P], U32, align_bytes=64)
            scales = step_pool.tile([P, STEP_PASSES * P], U8, align_bytes=64)
            operand_of[step] = (codes, scales)
            nc.vector.quantize_mx(
                out=codes[:, 0 : passes * P].bitcast(FP8X4),
                scales=scales[:, 0 : passes * P],
                in_=grouped_of[step][:, 0 : passes * PASS_VALUES],
            )

        spare = []

        def idle_passes(count):
            if not spare:
                sums = sums_pool.tile([P, STEP_PASSES, FEATURES], F32)
                spare.append(sums)
            for k in range(count):
                nc.tensor.matmul_mx(
                    out=spare[0][:, 0, :],
                    lhsT=w_codes[:].bitcast(FP8X4),
                    lhsT_scale=w_scales[:],
                    rhs=w_codes[:].bitcast(FP8X4),
                    rhs_scale=w_scales[:],
                    start=True,
                    stop=True,
                )

        def warm_up():
            sums = sums_pool.tile([P, STEP_PASSES, FEATURES], F32)
            for k in range(WARM_MATMULS):
                nc.tensor.matmul(
                    out=sums[:].rearrange("p k o -> p (k o)"), lhsT=ones[:], rhs=w_rows[:], start=True, stop=True
                )
            spare.append(sums)
            idle_passes(WARM_PASSES)

        def multiply(step):
            passes, sources = step
            codes, scales = operand_of[step]
            idle_passes(0)
            sums = spare.pop()
            for k in range(passes):
                columns = slice(k * P, (k + 1) * P)
                nc.tensor.matmul_mx(
                    out=sums[:, k, :],
                    lhsT=codes[:, columns].bitcast(FP8X4),
                    lhsT_scale=scales[:, columns],
                    rhs=w_codes[:].bitcast(FP8X4),
                    rhs_scale=w_scales[:],
                    start=True,
                    stop=True,
                )
            result = step_pool.tile([P, STEP_PASSES, FEATURES], F32)
            nc.vector.tensor_tensor(
                out=result[:, 0:passes, :],
                in0=sums[:, 0:passes, :],
                in1=bias[:].unsqueeze(1).to_broadcast([P, passes, FEATURES]),
                op=mybir.AluOpType.add,
            )
            for q, (g, first_row) in enumerate(sources):
                nc.sync.dma_start(
                    out=out_rows[g][:, first_row : first_row + passes, :],
                    in_=result[q:P:ROW_SETS, 0:passes, :],
                )

        nc.vector.quantize_mx(out=w_codes[:].bitcast(FP8X4), scales=w_scales[:], in_=w_grouped[:])
        for part in range(len(parts)):
            reorder(0, part)
            if part == 0:
                nc.scalar.copy(out=bias[:], in_=bias_sum[:, 0, :])
        warm_up()
        for i in range(len(steps) + MULTIPLY_LAG):
            if i >= MULTIPLY_LAG:
                multiply(steps[i - MULTIPLY_LAG])
            if i < len(steps):
                turn(steps[i])
                idle_passes(HOLD_PASSES - (STEP_PASSES if i >= MULTIPLY_LAG else 0))
            if 0 <= i - QUANTISE_LAG < len(steps):
                quantise(steps[i - QUANTISE_LAG])
            g, part = divmod(i, group_steps)
            if g + 1 < GROUPS and part < len(parts):
                reorder(g + 1, part)
